import numpy as np
import ml_dtypes

BF16 = ml_dtypes.bfloat16


def bf(x):
    return np.asarray(x, np.float32).astype(BF16)


def f32(x):
    return np.asarray(x, np.float32)


def f64(x):
    return np.asarray(x).astype(np.float64)


def striped(idx):
    return np.tile(idx.reshape(-1, 16).T, (8, 1))


S, D, M, K, N = 256, 128, 256, 8, 2048


def setup_inputs():
    idx = np.concatenate([np.random.permutation(S) for _ in range(K)])
    return {"table": bf(np.random.standard_normal((S, D))), "w_self": bf(np.random.standard_normal((D, M)) / np.sqrt(2 * D)), "w_diff": bf(np.random.standard_normal((D, M)) / np.sqrt(2 * D)), "b": f32(0.1 * np.random.standard_normal((M, 1))), "offs": striped(idx)}


def reference(table, w_self, w_diff, b, offs):
    idx = offs[:16].T.reshape(-1)
    t = f64(table).T
    ctr = f64(w_self).T @ t - f64(w_diff).T @ t + f64(b)
    e = (f64(w_diff).T @ t[:, idx]).reshape(M, K, S)
    return np.maximum(ctr[:, None, :] + e, 0.0).max(axis=1)

@@ -1,0 +1,74 @@
+import concourse.mybir as mybir
+from concourse.masks import make_identity
+
+BF16, F32, U16 = mybir.dt.bfloat16, mybir.dt.float32, mybir.dt.uint16
+RELU = mybir.ActivationFunctionType.Relu
+
+P = 128
+NODES = 256
+FEATURES = 128
+OUT_FEATURES = 256
+NEIGHBOURS = 8
+PIECE_COLUMNS = NODES // 16
+BANK = 2 * NODES
+
+FLOPS = 2 * FEATURES * OUT_FEATURES * (NEIGHBOURS * NODES + 2 * NODES)
+
+
+def tile_graphconv2d_kernel(tc, table, w_self, w_diff, b, offs, out):
+    nc = tc.nc
+    with (
+        tc.tile_pool(name="held", bufs=1) as held,
+        tc.tile_pool(name="work", bufs=2) as work,
+        tc.psum_pool(name="once", bufs=1) as once,
+        tc.psum_pool(name="banks", bufs=6) as banks,
+    ):
+        offsets = held.tile([P, NEIGHBOURS * PIECE_COLUMNS], U16, name="offsets")
+        nc.sync.dma_start(offsets[:], offs)
+        rows = held.tile([P, NODES // P, FEATURES], BF16, name="rows")
+        nc.scalar.dma_start(rows[:], table.rearrange("(h p) d -> p h d", p=P))
+        diff = held.tile([FEATURES, OUT_FEATURES], BF16, name="diff")
+        nc.scalar.dma_start(diff[:], w_diff)
+        own = held.tile([FEATURES, OUT_FEATURES], BF16, name="own")
+        nc.sync.dma_start(own[:], w_self)
+        bias = held.tile([P, OUT_FEATURES // P], F32, name="bias")
+        with nc.allow_non_contiguous_dma(reason="256 floats, one to a partition and block"):
+            nc.gpsimd.dma_start(bias[:], b.rearrange("(k p) o -> p (k o)", p=P))
+
+        identity = held.tile([P, P], BF16, name="identity")
+        make_identity(nc, identity[:])
+        flipped = once.tile([FEATURES, NODES], BF16, name="flipped")
+        for h in range(NODES // P):
+            nc.tensor.transpose(flipped[:, h * P : (h + 1) * P], rows[:, h, :], identity[:])
+        nodes = held.tile([FEATURES, NODES], BF16, name="nodes")
+        nc.vector.tensor_copy(nodes[:], flipped[:])
+
+        minus_diff = held.tile([FEATURES, OUT_FEATURES], BF16, name="minus_diff")
+        nc.gpsimd.tensor_scalar_mul(minus_diff[:], diff[:], -1.0)
+        centre = once.tile([P, OUT_FEATURES // P, NODES], F32, name="centre")
+        for k in range(OUT_FEATURES // P):
+            block = slice(k * P, (k + 1) * P)
+            nc.tensor.matmul(centre[:, k, :], own[:, block], nodes[:], start=True, stop=False)
+            nc.tensor.matmul(centre[:, k, :], minus_diff[:, block], nodes[:], start=False, stop=True)
+
+        for k in range(OUT_FEATURES // P):
+            block = slice(k * P, (k + 1) * P)
+            best = work.tile([P, BANK], F32, name="best")
+            for pair in range(NEIGHBOURS // 2):
+                bank = banks.tile([P, BANK], F32, name="bank")
+                for half in range(2):
+                    t = 2 * pair + half
+                    picked = nodes[:].indirect(offsets[:, t * PIECE_COLUMNS : (t + 1) * PIECE_COLUMNS])
+                    nc.tensor.matmul(
+                        bank[:, half * NODES : (half + 1) * NODES], diff[:, block], picked, start=True, stop=True
+                    )
+                if pair == 0:
+                    nc.scalar.copy(best[:], bank[:])
+                else:
+                    nc.vector.tensor_max(best[:], best[:], bank[:])
+            top = work.tile([P, NODES], F32, name="top")
+            nc.vector.tensor_max(top[:], best[:, :NODES], best[:, NODES:])
+            nc.vector.tensor_add(top[:], top[:], centre[:, k, :])
+            result = work.tile([P, NODES], F32, name="result")
+            nc.scalar.activation(result[:], top[:], RELU, bias=bias[:, k : k + 1])
+            nc.sync.dma_start(out[block, :], result[:])

@@ -2,7 +2,7 @@ import concourse.mybir as mybir
 from concourse.masks import make_identity
 
 BF16, F32, U16 = mybir.dt.bfloat16, mybir.dt.float32, mybir.dt.uint16
-RELU = mybir.ActivationFunctionType.Relu
+ADD, MAX = mybir.AluOpType.add, mybir.AluOpType.max
 
 P = 128
 NODES = 256
@@ -10,7 +10,7 @@ FEATURES = 128
 OUT_FEATURES = 256
 NEIGHBOURS = 8
 PIECE_COLUMNS = NODES // 16
-BANK = 2 * NODES
+BLOCKS = OUT_FEATURES // P
 
 FLOPS = 2 * FEATURES * OUT_FEATURES * (NEIGHBOURS * NODES + 2 * NODES)
 
@@ -19,10 +19,12 @@ def tile_graphconv2d_kernel(tc, table, w_self, w_diff, b, offs, out):
     nc = tc.nc
     with (
         tc.tile_pool(name="held", bufs=1) as held,
-        tc.tile_pool(name="work", bufs=2) as work,
         tc.psum_pool(name="once", bufs=1) as once,
-        tc.psum_pool(name="banks", bufs=6) as banks,
+        tc.psum_pool(name="products", bufs=6) as products,
     ):
+        identity = held.tile([P, P], BF16, name="identity")
+        make_identity(nc, identity[:])
+
         offsets = held.tile([P, NEIGHBOURS * PIECE_COLUMNS], U16, name="offsets")
         nc.sync.dma_start(offsets[:], offs)
         rows = held.tile([P, NODES // P, FEATURES], BF16, name="rows")
@@ -31,12 +33,10 @@ def tile_graphconv2d_kernel(tc, table, w_self, w_diff, b, offs, out):
         nc.scalar.dma_start(diff[:], w_diff)
         own = held.tile([FEATURES, OUT_FEATURES], BF16, name="own")
         nc.sync.dma_start(own[:], w_self)
-        bias = held.tile([P, OUT_FEATURES // P], F32, name="bias")
+        bias = held.tile([P, BLOCKS], F32, name="bias")
         with nc.allow_non_contiguous_dma(reason="256 floats, one to a partition and block"):
-            nc.gpsimd.dma_start(bias[:], b.rearrange("(k p) o -> p (k o)", p=P))
+            nc.sync.dma_start(bias[:], b.rearrange("(k p) o -> p (k o)", p=P))
 
-        identity = held.tile([P, P], BF16, name="identity")
-        make_identity(nc, identity[:])
         flipped = once.tile([FEATURES, NODES], BF16, name="flipped")
         for h in range(NODES // P):
             nc.tensor.transpose(flipped[:, h * P : (h + 1) * P], rows[:, h, :], identity[:])
@@ -44,31 +44,27 @@ def tile_graphconv2d_kernel(tc, table, w_self, w_diff, b, offs, out):
         nc.vector.tensor_copy(nodes[:], flipped[:])
 
         minus_diff = held.tile([FEATURES, OUT_FEATURES], BF16, name="minus_diff")
-        nc.gpsimd.tensor_scalar_mul(minus_diff[:], diff[:], -1.0)
-        centre = once.tile([P, OUT_FEATURES // P, NODES], F32, name="centre")
-        for k in range(OUT_FEATURES // P):
+        nc.scalar.mul(minus_diff[:], diff[:], -1.0)
+        centre = once.tile([P, BLOCKS, NODES], F32, name="centre")
+        for k in range(BLOCKS):
             block = slice(k * P, (k + 1) * P)
             nc.tensor.matmul(centre[:, k, :], own[:, block], nodes[:], start=True, stop=False)
             nc.tensor.matmul(centre[:, k, :], minus_diff[:, block], nodes[:], start=False, stop=True)
 
-        for k in range(OUT_FEATURES // P):
-            block = slice(k * P, (k + 1) * P)
-            best = work.tile([P, BANK], F32, name="best")
-            for pair in range(NEIGHBOURS // 2):
-                bank = banks.tile([P, BANK], F32, name="bank")
-                for half in range(2):
-                    t = 2 * pair + half
-                    picked = nodes[:].indirect(offsets[:, t * PIECE_COLUMNS : (t + 1) * PIECE_COLUMNS])
-                    nc.tensor.matmul(
-                        bank[:, half * NODES : (half + 1) * NODES], diff[:, block], picked, start=True, stop=True
-                    )
-                if pair == 0:
-                    nc.scalar.copy(best[:], bank[:])
+        best = [held.tile([P, NODES], F32, name=f"best{k}") for k in range(BLOCKS)]
+        for t in range(NEIGHBOURS):
+            picked = nodes[:].indirect(offsets[:, t * PIECE_COLUMNS : (t + 1) * PIECE_COLUMNS])
+            for k in range(BLOCKS):
+                product = products.tile([P, NODES], F32, name="product")
+                nc.tensor.matmul(product[:], diff[:, k * P : (k + 1) * P], picked, start=True, stop=True)
+                if t == 0:
+                    nc.scalar.copy(best[k][:], product[:])
                 else:
-                    nc.vector.tensor_max(best[:], best[:], bank[:])
-            top = work.tile([P, NODES], F32, name="top")
-            nc.vector.tensor_max(top[:], best[:, :NODES], best[:, NODES:])
-            nc.vector.tensor_add(top[:], top[:], centre[:, k, :])
-            result = work.tile([P, NODES], F32, name="result")
-            nc.scalar.activation(result[:], top[:], RELU, bias=bias[:, k : k + 1])
-            nc.sync.dma_start(out[block, :], result[:])
+                    nc.vector.tensor_max(best[k][:], best[k][:], product[:])
+
+        for k in range(BLOCKS):
+            nc.vector.tensor_add(best[k][:], best[k][:], centre[:, k, :])
+        for k in range(BLOCKS):
+            nc.vector.tensor_scalar(best[k][:], best[k][:], bias[:, k : k + 1], 0.0, ADD, MAX)
+            store_queue = nc.sync if k == 0 else nc.scalar
+            store_queue.dma_start(out[k * P : (k + 1) * P, :], best[k][:])

@@ -11,6 +11,8 @@ OUT_FEATURES = 256
 NEIGHBOURS = 8
 PIECE_COLUMNS = NODES // 16
 BLOCKS = OUT_FEATURES // P
+BANK = 512
+WARM_UPS = 4
 
 FLOPS = 2 * FEATURES * OUT_FEATURES * (NEIGHBOURS * NODES + 2 * NODES)
 
@@ -24,6 +26,12 @@ def tile_graphconv2d_kernel(tc, table, w_self, w_diff, b, offs, out):
     ):
         identity = held.tile([P, P], BF16, name="identity")
         make_identity(nc, identity[:])
+
+        zeros = held.tile([P, BANK], BF16, name="zeros")
+        nc.vector.memset(zeros[:], 0.0)
+        unread = products.tile([P, BANK], F32, name="unread", tag="product")
+        for warm_up in range(WARM_UPS):
+            nc.tensor.matmul(unread[:], zeros[:, :P], zeros[:], start=True, stop=True)
 
         offsets = held.tile([P, NEIGHBOURS * PIECE_COLUMNS], U16, name="offsets")
         nc.sync.dma_start(offsets[:], offs)
@@ -55,7 +63,7 @@ def tile_graphconv2d_kernel(tc, table, w_self, w_diff, b, offs, out):
         for t in range(NEIGHBOURS):
             picked = nodes[:].indirect(offsets[:, t * PIECE_COLUMNS : (t + 1) * PIECE_COLUMNS])
             for k in range(BLOCKS):
-                product = products.tile([P, NODES], F32, name="product")
+                product = products.tile([P, NODES], F32, name="product", tag="product")
                 nc.tensor.matmul(product[:], diff[:, k * P : (k + 1) * P], picked, start=True, stop=True)
                 if t == 0:
                     nc.scalar.copy(best[k][:], product[:])

@@ -11,8 +11,6 @@ OUT_FEATURES = 256
 NEIGHBOURS = 8
 PIECE_COLUMNS = NODES // 16
 BLOCKS = OUT_FEATURES // P
-BANK = 512
-WARM_UPS = 4
 
 FLOPS = 2 * FEATURES * OUT_FEATURES * (NEIGHBOURS * NODES + 2 * NODES)
 
@@ -22,16 +20,10 @@ def tile_graphconv2d_kernel(tc, table, w_self, w_diff, b, offs, out):
     with (
         tc.tile_pool(name="held", bufs=1) as held,
         tc.psum_pool(name="once", bufs=1) as once,
-        tc.psum_pool(name="products", bufs=6) as products,
+        tc.psum_pool(name="products", bufs=7) as products,
     ):
         identity = held.tile([P, P], BF16, name="identity")
         make_identity(nc, identity[:])
-
-        zeros = held.tile([P, BANK], BF16, name="zeros")
-        nc.vector.memset(zeros[:], 0.0)
-        unread = products.tile([P, BANK], F32, name="unread", tag="product")
-        for warm_up in range(WARM_UPS):
-            nc.tensor.matmul(unread[:], zeros[:, :P], zeros[:], start=True, stop=True)
 
         offsets = held.tile([P, NEIGHBOURS * PIECE_COLUMNS], U16, name="offsets")
         nc.sync.dma_start(offsets[:], offs)
@@ -51,14 +43,6 @@ def tile_graphconv2d_kernel(tc, table, w_self, w_diff, b, offs, out):
         nodes = held.tile([FEATURES, NODES], BF16, name="nodes")
         nc.vector.tensor_copy(nodes[:], flipped[:])
 
-        minus_diff = held.tile([FEATURES, OUT_FEATURES], BF16, name="minus_diff")
-        nc.scalar.mul(minus_diff[:], diff[:], -1.0)
-        centre = once.tile([P, BLOCKS, NODES], F32, name="centre")
-        for k in range(BLOCKS):
-            block = slice(k * P, (k + 1) * P)
-            nc.tensor.matmul(centre[:, k, :], own[:, block], nodes[:], start=True, stop=False)
-            nc.tensor.matmul(centre[:, k, :], minus_diff[:, block], nodes[:], start=False, stop=True)
-
         best = [held.tile([P, NODES], F32, name=f"best{k}") for k in range(BLOCKS)]
         for t in range(NEIGHBOURS):
             picked = nodes[:].indirect(offsets[:, t * PIECE_COLUMNS : (t + 1) * PIECE_COLUMNS])
@@ -70,8 +54,15 @@ def tile_graphconv2d_kernel(tc, table, w_self, w_diff, b, offs, out):
                 else:
                     nc.vector.tensor_max(best[k][:], best[k][:], product[:])
 
+        minus_diff = held.tile([FEATURES, OUT_FEATURES], BF16, name="minus_diff")
+        nc.scalar.mul(minus_diff[:], diff[:], -1.0)
         for k in range(BLOCKS):
-            nc.vector.tensor_add(best[k][:], best[k][:], centre[:, k, :])
+            block = slice(k * P, (k + 1) * P)
+            centre = products.tile([P, NODES], F32, name="centre", tag="product")
+            nc.tensor.matmul(centre[:], own[:, block], nodes[:], start=True, stop=False)
+            nc.tensor.matmul(centre[:], minus_diff[:, block], nodes[:], start=False, stop=True)
+            nc.vector.tensor_add(best[k][:], best[k][:], centre[:])
+
         for k in range(BLOCKS):
             nc.vector.tensor_scalar(best[k][:], best[k][:], bias[:, k : k + 1], 0.0, ADD, MAX)
             store_queue = nc.sync if k == 0 else nc.scalar

@@ -50,12 +50,12 @@ def tile_graphconv2d_kernel(tc, table, w_self, w_diff, b, offs, out):
                 product = products.tile([P, NODES], F32, name="product", tag="product")
                 nc.tensor.matmul(product[:], diff[:, k * P : (k + 1) * P], picked, start=True, stop=True)
                 if t == 0:
-                    nc.scalar.copy(best[k][:], product[:])
+                    nc.vector.tensor_copy(best[k][:], product[:])
                 else:
                     nc.vector.tensor_max(best[k][:], best[k][:], product[:])
 
         minus_diff = held.tile([FEATURES, OUT_FEATURES], BF16, name="minus_diff")
-        nc.scalar.mul(minus_diff[:], diff[:], -1.0)
+        nc.gpsimd.tensor_scalar_mul(minus_diff[:], diff[:], -1.0)
         for k in range(BLOCKS):
             block = slice(k * P, (k + 1) * P)
             centre = products.tile([P, NODES], F32, name="centre", tag="product")

@@ -11,6 +11,8 @@ OUT_FEATURES = 256
 NEIGHBOURS = 8
 PIECE_COLUMNS = NODES // 16
 BLOCKS = OUT_FEATURES // P
+BANK = 512
+WARM_UPS = 3
 
 FLOPS = 2 * FEATURES * OUT_FEATURES * (NEIGHBOURS * NODES + 2 * NODES)
 
@@ -24,6 +26,12 @@ def tile_graphconv2d_kernel(tc, table, w_self, w_diff, b, offs, out):
     ):
         identity = held.tile([P, P], BF16, name="identity")
         make_identity(nc, identity[:])
+
+        zeros = held.tile([P, BANK], BF16, name="zeros")
+        nc.vector.memset(zeros[:], 0.0)
+        unread = products.tile([P, BANK], F32, name="unread", tag="product")
+        for warm_up in range(WARM_UPS):
+            nc.tensor.matmul(unread[:], zeros[:, :P], zeros[:], start=True, stop=True)
 
         offsets = held.tile([P, NEIGHBOURS * PIECE_COLUMNS], U16, name="offsets")
         nc.sync.dma_start(offsets[:], offs)

@@ -12,6 +12,7 @@ NEIGHBOURS = 8
 PIECE_COLUMNS = NODES // 16
 BLOCKS = OUT_FEATURES // P
 BANK = 512
+PARTS = 2
 WARM_UPS = 3
 
 FLOPS = 2 * FEATURES * OUT_FEATURES * (NEIGHBOURS * NODES + 2 * NODES)
@@ -52,15 +53,17 @@ def tile_graphconv2d_kernel(tc, table, w_self, w_diff, b, offs, out):
         nc.vector.tensor_copy(nodes[:], flipped[:])
 
         best = [held.tile([P, NODES], F32, name=f"best{k}") for k in range(BLOCKS)]
+        parts = [slice(i * NODES // PARTS, (i + 1) * NODES // PARTS) for i in range(PARTS)]
         for t in range(NEIGHBOURS):
             picked = nodes[:].indirect(offsets[:, t * PIECE_COLUMNS : (t + 1) * PIECE_COLUMNS])
             for k in range(BLOCKS):
                 product = products.tile([P, NODES], F32, name="product", tag="product")
                 nc.tensor.matmul(product[:], diff[:, k * P : (k + 1) * P], picked, start=True, stop=True)
-                if t == 0:
-                    nc.vector.tensor_copy(best[k][:], product[:])
-                else:
-                    nc.vector.tensor_max(best[k][:], best[k][:], product[:])
+                for part in parts:
+                    if t == 0:
+                        nc.vector.tensor_copy(best[k][:, part], product[:, part])
+                    else:
+                        nc.vector.tensor_max(best[k][:, part], best[k][:, part], product[:, part])
 
         minus_diff = held.tile([FEATURES, OUT_FEATURES], BF16, name="minus_diff")
         nc.gpsimd.tensor_scalar_mul(minus_diff[:], diff[:], -1.0)
@@ -69,7 +72,8 @@ def tile_graphconv2d_kernel(tc, table, w_self, w_diff, b, offs, out):
             centre = products.tile([P, NODES], F32, name="centre", tag="product")
             nc.tensor.matmul(centre[:], own[:, block], nodes[:], start=True, stop=False)
             nc.tensor.matmul(centre[:], minus_diff[:, block], nodes[:], start=False, stop=True)
-            nc.vector.tensor_add(best[k][:], best[k][:], centre[:])
+            for part in parts:
+                nc.vector.tensor_add(best[k][:, part], best[k][:, part], centre[:, part])
 
         for k in range(BLOCKS):
             nc.vector.tensor_scalar(best[k][:], best[k][:], bias[:, k : k + 1], 0.0, ADD, MAX)

@@ -2,7 +2,7 @@ import concourse.mybir as mybir
 from concourse.masks import make_identity
 
 BF16, F32, U16 = mybir.dt.bfloat16, mybir.dt.float32, mybir.dt.uint16
-ADD, MAX = mybir.AluOpType.add, mybir.AluOpType.max
+IDENTITY = mybir.ActivationFunctionType.Identity
 
 P = 128
 NODES = 256
@@ -52,6 +52,18 @@ def tile_graphconv2d_kernel(tc, table, w_self, w_diff, b, offs, out):
         nodes = held.tile([FEATURES, NODES], BF16, name="nodes")
         nc.vector.tensor_copy(nodes[:], flipped[:])
 
+        minus_diff = held.tile([FEATURES, OUT_FEATURES], BF16, name="minus_diff")
+        nc.scalar.mul(minus_diff[:], diff[:], -1.0)
+        minus_bias = held.tile([P, BLOCKS], F32, name="minus_bias")
+        nc.gpsimd.tensor_scalar_mul(minus_bias[:], bias[:], -1.0)
+        floor = [held.tile([P, NODES], F32, name=f"floor{k}") for k in range(BLOCKS)]
+        for k in range(BLOCKS):
+            block = slice(k * P, (k + 1) * P)
+            centre = products.tile([P, NODES], F32, name="centre", tag="product")
+            nc.tensor.matmul(centre[:], own[:, block], nodes[:], start=True, stop=False)
+            nc.tensor.matmul(centre[:], minus_diff[:, block], nodes[:], start=False, stop=True)
+            nc.scalar.activation(floor[k][:], centre[:], IDENTITY, bias=minus_bias[:, k : k + 1], scale=-1.0)
+
         best = [held.tile([P, NODES], F32, name=f"best{k}") for k in range(BLOCKS)]
         parts = [slice(i * NODES // PARTS, (i + 1) * NODES // PARTS) for i in range(PARTS)]
         for t in range(NEIGHBOURS):
@@ -59,23 +71,12 @@ def tile_graphconv2d_kernel(tc, table, w_self, w_diff, b, offs, out):
             for k in range(BLOCKS):
                 product = products.tile([P, NODES], F32, name="product", tag="product")
                 nc.tensor.matmul(product[:], diff[:, k * P : (k + 1) * P], picked, start=True, stop=True)
+                so_far = floor[k] if t == 0 else best[k]
                 for part in parts:
-                    if t == 0:
-                        nc.vector.tensor_copy(best[k][:, part], product[:, part])
-                    else:
-                        nc.vector.tensor_max(best[k][:, part], best[k][:, part], product[:, part])
+                    nc.vector.tensor_max(best[k][:, part], so_far[:, part], product[:, part])
 
-        minus_diff = held.tile([FEATURES, OUT_FEATURES], BF16, name="minus_diff")
-        nc.gpsimd.tensor_scalar_mul(minus_diff[:], diff[:], -1.0)
         for k in range(BLOCKS):
-            block = slice(k * P, (k + 1) * P)
-            centre = products.tile([P, NODES], F32, name="centre", tag="product")
-            nc.tensor.matmul(centre[:], own[:, block], nodes[:], start=True, stop=False)
-            nc.tensor.matmul(centre[:], minus_diff[:, block], nodes[:], start=False, stop=True)
             for part in parts:
-                nc.vector.tensor_add(best[k][:, part], best[k][:, part], centre[:, part])
-
-        for k in range(BLOCKS):
-            nc.vector.tensor_scalar(best[k][:], best[k][:], bias[:, k : k + 1], 0.0, ADD, MAX)
+                nc.vector.tensor_sub(best[k][:, part], best[k][:, part], floor[k][:, part])
             store_queue = nc.sync if k == 0 else nc.scalar
             store_queue.dma_start(out[k * P : (k + 1) * P, :], best[k][:])

@@ -78,5 +78,7 @@ def tile_graphconv2d_kernel(tc, table, w_self, w_diff, b, offs, out):
         for k in range(BLOCKS):
             for part in parts:
                 nc.vector.tensor_sub(best[k][:, part], best[k][:, part], floor[k][:, part])
-            store_queue = nc.sync if k == 0 else nc.scalar
-            store_queue.dma_start(out[k * P : (k + 1) * P, :], best[k][:])
+                if k == BLOCKS - 1:
+                    nc.scalar.dma_start(out[k * P : (k + 1) * P, part], best[k][:, part])
+            if k < BLOCKS - 1:
+                nc.sync.dma_start(out[k * P : (k + 1) * P, :], best[k][:])

@@ -13,6 +13,7 @@ PIECE_COLUMNS = NODES // 16
 BLOCKS = OUT_FEATURES // P
 BANK = 512
 PARTS = 2
+FILLS = 2
 WARM_UPS = 3
 
 FLOPS = 2 * FEATURES * OUT_FEATURES * (NEIGHBOURS * NODES + 2 * NODES)
@@ -49,6 +50,8 @@ def tile_graphconv2d_kernel(tc, table, w_self, w_diff, b, offs, out):
         flipped = once.tile([FEATURES, NODES], BF16, name="flipped")
         for h in range(NODES // P):
             nc.tensor.transpose(flipped[:, h * P : (h + 1) * P], rows[:, h, :], identity[:])
+        for fill in range(FILLS):
+            nc.tensor.matmul(unread[:, :NODES], identity[:], rows[:], start=True, stop=True)
         nodes = held.tile([FEATURES, NODES], BF16, name="nodes")
         nc.vector.tensor_copy(nodes[:], flipped[:])
 

import concourse.mybir as mybir
from concourse.masks import make_identity

BF16, F32, U16 = mybir.dt.bfloat16, mybir.dt.float32, mybir.dt.uint16
IDENTITY = mybir.ActivationFunctionType.Identity

P = 128
NODES = 256
FEATURES = 128
OUT_FEATURES = 256
NEIGHBOURS = 8
PIECE_COLUMNS = NODES // 16
BLOCKS = OUT_FEATURES // P
BANK = 512
PARTS = 2
FILLS = 2
WARM_UPS = 3

FLOPS = 2 * FEATURES * OUT_FEATURES * (NEIGHBOURS * NODES + 2 * NODES)


def tile_graphconv2d_kernel(tc, table, w_self, w_diff, b, offs, out):
    nc = tc.nc
    with (
        tc.tile_pool(name="held", bufs=1) as held,
        tc.psum_pool(name="once", bufs=1) as once,
        tc.psum_pool(name="products", bufs=7) as products,
    ):
        identity = held.tile([P, P], BF16, name="identity")
        make_identity(nc, identity[:])

        zeros = held.tile([P, BANK], BF16, name="zeros")
        nc.vector.memset(zeros[:], 0.0)
        unread = products.tile([P, BANK], F32, name="unread", tag="product")
        for warm_up in range(WARM_UPS):
            nc.tensor.matmul(unread[:], zeros[:, :P], zeros[:], start=True, stop=True)

        offsets = held.tile([P, NEIGHBOURS * PIECE_COLUMNS], U16, name="offsets")
        nc.sync.dma_start(offsets[:], offs)
        rows = held.tile([P, NODES // P, FEATURES], BF16, name="rows")
        nc.scalar.dma_start(rows[:], table.rearrange("(h p) d -> p h d", p=P))
        diff = held.tile([FEATURES, OUT_FEATURES], BF16, name="diff")
        nc.scalar.dma_start(diff[:], w_diff)
        own = held.tile([FEATURES, OUT_FEATURES], BF16, name="own")
        nc.sync.dma_start(own[:], w_self)
        bias = held.tile([P, BLOCKS], F32, name="bias")
        with nc.allow_non_contiguous_dma(reason="256 floats, one to a partition and block"):
            nc.sync.dma_start(bias[:], b.rearrange("(k p) o -> p (k o)", p=P))

        flipped = once.tile([FEATURES, NODES], BF16, name="flipped")
        for h in range(NODES // P):
            nc.tensor.transpose(flipped[:, h * P : (h + 1) * P], rows[:, h, :], identity[:])
        for fill in range(FILLS):
            nc.tensor.matmul(unread[:, :NODES], identity[:], rows[:], start=True, stop=True)
        nodes = held.tile([FEATURES, NODES], BF16, name="nodes")
        nc.vector.tensor_copy(nodes[:], flipped[:])

        minus_diff = held.tile([FEATURES, OUT_FEATURES], BF16, name="minus_diff")
        nc.scalar.mul(minus_diff[:], diff[:], -1.0)
        minus_bias = held.tile([P, BLOCKS], F32, name="minus_bias")
        nc.gpsimd.tensor_scalar_mul(minus_bias[:], bias[:], -1.0)
        floor = [held.tile([P, NODES], F32, name=f"floor{k}") for k in range(BLOCKS)]
        for k in range(BLOCKS):
            block = slice(k * P, (k + 1) * P)
            centre = products.tile([P, NODES], F32, name="centre", tag="product")
            nc.tensor.matmul(centre[:], own[:, block], nodes[:], start=True, stop=False)
            nc.tensor.matmul(centre[:], minus_diff[:, block], nodes[:], start=False, stop=True)
            nc.scalar.activation(floor[k][:], centre[:], IDENTITY, bias=minus_bias[:, k : k + 1], scale=-1.0)

        best = [held.tile([P, NODES], F32, name=f"best{k}") for k in range(BLOCKS)]
        parts = [slice(i * NODES // PARTS, (i + 1) * NODES // PARTS) for i in range(PARTS)]
        for t in range(NEIGHBOURS):
            picked = nodes[:].indirect(offsets[:, t * PIECE_COLUMNS : (t + 1) * PIECE_COLUMNS])
            for k in range(BLOCKS):
                product = products.tile([P, NODES], F32, name="product", tag="product")
                nc.tensor.matmul(product[:], diff[:, k * P : (k + 1) * P], picked, start=True, stop=True)
                so_far = floor[k] if t == 0 else best[k]
                for part in parts:
                    nc.vector.tensor_max(best[k][:, part], so_far[:, part], product[:, part])

        for k in range(BLOCKS):
            for part in parts:
                nc.vector.tensor_sub(best[k][:, part], best[k][:, part], floor[k][:, part])
                if k == BLOCKS - 1:
                    nc.scalar.dma_start(out[k * P : (k + 1) * P, part], best[k][:, part])
            if k < BLOCKS - 1:
                nc.sync.dma_start(out[k * P : (k + 1) * P, :], best[k][:])
